import numpy as np
import ml_dtypes


def mxq(x, axis, fmt="e4m3"):
    dtype, down = {"e4m3": (ml_dtypes.float8_e4m3fn, 7), "e5m2": (ml_dtypes.float8_e5m2, 14)}[fmt]
    v = np.moveaxis(np.asarray(x, np.float32).astype(ml_dtypes.bfloat16).astype(np.float64), axis, -1)
    blocks = v.reshape(v.shape[:-1] + (-1, 32))
    amax = np.abs(blocks).max(-1, keepdims=True)
    byte = np.maximum(np.where(amax > 0, np.frexp(amax)[1] - 1 + 127, 0) - down, 1)
    scale = np.exp2(byte - 127.0)
    codes = (blocks / scale).astype(np.float32).astype(dtype).astype(np.float64)
    return np.moveaxis((codes * scale).reshape(v.shape), -1, axis)


WIDE = False


def mx_kscale(k):
    if not WIDE:
        return np.ones(k)
    levels = np.array([10, -10, 5, -5, 0])
    a = np.random.permutation(np.resize(levels, k // 512 * 4)).reshape(k // 512, 4)
    idx = np.arange(k)
    return np.exp2(a[idx // 512, idx % 128 // 32])


BF16 = ml_dtypes.bfloat16


def bf(x):
    return np.asarray(x, np.float32).astype(BF16)


def f64(x):
    return np.asarray(x).astype(np.float64)


B, S, HID, NH, NKV, HD, FF = 1, 512, 2048, 16, 4, 128, 8192
T = B * S
EPS = 1e-6


def rms(u, w):
    return u * (1.0 / np.sqrt(np.mean(u * u, axis=-1, keepdims=True) + EPS)) * w


def rotate_half(u):
    u1, u2 = np.split(u, 2, axis=-1)
    return np.concatenate([-u2, u1], axis=-1)


def setup_inputs():
    s = mx_kscale(HID)
    pos = np.tile(np.arange(S, dtype=np.float64), B)
    inv_freq = 1.0 / (10000.0 ** (np.arange(0, HD, 2, dtype=np.float64) / HD))
    ang = pos[:, None] * inv_freq[None, :]
    emb = np.concatenate([ang, ang], axis=-1)
    a = 1.0 / np.sqrt(HID)
    return {"x": bf(np.random.standard_normal((T, HID)) * 0.5),
            "cos": bf(np.cos(emb)),
            "sin": bf(np.sin(emb)),
            "wq": bf(np.random.standard_normal((NH * HD, HID)) * a / s[None, :]),
            "bq": bf(np.random.standard_normal(NH * HD) * 0.3),
            "wk": bf(np.random.standard_normal((NKV * HD, HID)) * a / s[None, :]),
            "bk": bf(np.random.standard_normal(NKV * HD) * 0.3),
            "wv": bf(np.random.standard_normal((NKV * HD, HID)) * 2.0 * a / s[None, :]),
            "bv": bf(np.random.standard_normal(NKV * HD) * 0.3),
            "q_norm_w": bf(1.0 + 0.1 * np.random.standard_normal(HD)),
            "k_norm_w": bf(1.0 + 0.1 * np.random.standard_normal(HD)),
            "ln1_w": bf((1.0 + 0.1 * np.random.standard_normal(HID)) * s)}


def reference(x, cos, sin, wq, bq, wk, bk, wv, bv, q_norm_w, k_norm_w, ln1_w):
    h = rms(f64(x), f64(ln1_w))
    hq = mxq(h, 1, "e4m3")
    q = ((hq @ mxq(f64(wq), 1, "e4m3").T) + f64(bq)).reshape(T, NH, HD)
    k = ((hq @ mxq(f64(wk), 1, "e4m3").T) + f64(bk)).reshape(T, NKV, HD)
    v = ((hq @ mxq(f64(wv), 1, "e4m3").T) + f64(bv)).reshape(T, NKV, HD)
    q = rms(q, f64(q_norm_w))
    k = rms(k, f64(k_norm_w))
    c, sn = f64(cos)[:, None, :], f64(sin)[:, None, :]
    q = q * c + rotate_half(q) * sn
    k = k * c + rotate_half(k) * sn
    return q, k, v

@@ -1,0 +1,339 @@
+from contextlib import ExitStack
+
+import concourse.mybir as mybir
+from concourse.masks import make_identity
+
+F32 = mybir.dt.float32
+BF16 = mybir.dt.bfloat16
+U32 = mybir.dt.uint32
+U8 = mybir.dt.uint8
+FP8X4 = mybir.dt.float8_e4m3fn_x4
+ACT = mybir.ActivationFunctionType
+ALU = mybir.AluOpType
+
+P = 128
+TOKENS = 512
+HID = 2048
+HEAD = 128
+HALF = HEAD // 2
+EPS = 1e-6
+
+TOKEN_TILES = TOKENS // P
+PACK = 4
+K_PASS = P * PACK
+PASSES = HID // K_PASS
+GROUP = 512
+GROUP_HEADS = GROUP // HEAD
+ROW_TILES = GROUP // P
+Q_GROUPS = 4
+K_GROUP = 4
+V_GROUP = 5
+GROUPS = 6
+WEIGHT_BUFS = 4
+
+FLOPS = 2 * TOKENS * HID * GROUPS * GROUP
+
+
+def tile_qwen2decoderlayer_pa_kernel(
+    tc, x, cos, sin, wq, bq, wk, bk, wv, bv, q_norm_w, k_norm_w, ln1_w, out_0, out_1, out_2
+):
+    nc = tc.nc
+
+    weight_rows = [wq[n * GROUP : (n + 1) * GROUP, :] for n in range(Q_GROUPS)] + [wk, wv]
+    q_flat = out_0.rearrange("t h d -> t (h d)")
+    out_cols = [q_flat[:, n * GROUP : (n + 1) * GROUP] for n in range(Q_GROUPS)] + [
+        out_1.rearrange("t h d -> t (h d)"),
+        out_2.rearrange("t h d -> t (h d)"),
+    ]
+
+    with ExitStack() as ctx:
+        const = ctx.enter_context(tc.tile_pool(name="const", bufs=1))
+        hpool = ctx.enter_context(tc.tile_pool(name="hpool", bufs=2))
+        wpool = ctx.enter_context(tc.tile_pool(name="wpool", bufs=WEIGHT_BUFS))
+        gpool = ctx.enter_context(tc.tile_pool(name="gpool", bufs=6))
+        cpool = ctx.enter_context(tc.tile_pool(name="cpool", bufs=2))
+        epool = ctx.enter_context(tc.tile_pool(name="epool", bufs=2))
+        scratch = ctx.enter_context(tc.tile_pool(name="scratch", bufs=1))
+        stats = ctx.enter_context(tc.tile_pool(name="stats", bufs=2))
+        acc_psum = ctx.enter_context(tc.psum_pool(name="acc_psum", bufs=4))
+        tp_psum = ctx.enter_context(tc.psum_pool(name="tp_psum", bufs=4))
+
+        x_sb = const.tile([P, TOKEN_TILES, HID], BF16)
+        lnw = const.tile([P, HID], BF16)
+        nc.sync.dma_start(out=x_sb[:, 0, :], in_=x[0:P, :])
+        nc.sync.dma_start(out=lnw[:], in_=ln1_w.partition_broadcast(P))
+        for i in range(1, TOKEN_TILES):
+            nc.sync.dma_start(out=x_sb[:, i, :], in_=x[i * P : (i + 1) * P, :])
+
+        w_sb = {}
+
+        def load_weights(n):
+            w_rows = wpool.tile([P, ROW_TILES, HID], BF16)
+            nc.sync.dma_start(out=w_rows[:], in_=weight_rows[n].rearrange("(r p) k -> p r k", p=P))
+            w_sb[n] = w_rows
+
+        load_weights(0)
+        load_weights(1)
+        cos_sb = const.tile([P, TOKEN_TILES, HEAD], BF16)
+        nc.sync.dma_start(out=cos_sb[:], in_=cos.rearrange("(i p) d -> p i d", p=P))
+        sin_sb = const.tile([P, TOKEN_TILES, HEAD], BF16)
+        nc.sync.dma_start(out=sin_sb[:], in_=sin.rearrange("(i p) d -> p i d", p=P))
+        gain_q = const.tile([P, HEAD], BF16)
+        nc.sync.dma_start(out=gain_q[:], in_=q_norm_w.partition_broadcast(P))
+        gain_k = const.tile([P, HEAD], BF16)
+        nc.sync.dma_start(out=gain_k[:], in_=k_norm_w.partition_broadcast(P))
+        bias = const.tile([P, GROUPS * GROUP], BF16)
+        nc.sync.dma_start(out=bias[:, 0 : Q_GROUPS * GROUP], in_=bq.partition_broadcast(P))
+        nc.sync.dma_start(
+            out=bias[:, K_GROUP * GROUP : (K_GROUP + 1) * GROUP], in_=bk.partition_broadcast(P)
+        )
+        nc.sync.dma_start(
+            out=bias[:, V_GROUP * GROUP : (V_GROUP + 1) * GROUP], in_=bv.partition_broadcast(P)
+        )
+        for n in range(2, WEIGHT_BUFS):
+            load_weights(n)
+
+        ident_bf = const.tile([P, P], BF16)
+        make_identity(nc, ident_bf[:])
+        ident_f = const.tile([P, P], F32)
+        make_identity(nc, ident_f[:])
+        eps = const.tile([P, 1], F32)
+        nc.vector.memset(eps[:], EPS)
+        warm = const.tile([P, 1], F32)
+        nc.scalar.activation(out=warm[:], in_=eps[:], func=ACT.Sqrt)
+        squares = const.tile([P, HID], BF16)
+
+        def rope_tables(gain, name):
+            swapped = const.tile([P, HEAD], BF16, name="swapped_" + name)
+            nc.gpsimd.tensor_scalar(
+                out=swapped[:, 0:HALF], in0=gain[:, HALF:HEAD], scalar1=-1.0, scalar2=0.0,
+                op0=ALU.mult, op1=ALU.add,
+            )
+            nc.gpsimd.tensor_scalar(
+                out=swapped[:, HALF:HEAD], in0=gain[:, 0:HALF], scalar1=1.0, scalar2=0.0,
+                op0=ALU.mult, op1=ALU.add,
+            )
+            cos_gain = const.tile([P, TOKEN_TILES, HEAD], F32, name="cos_gain_" + name)
+            nc.gpsimd.tensor_tensor(
+                out=cos_gain[:], in0=cos_sb[:],
+                in1=gain[:].unsqueeze(1).to_broadcast([P, TOKEN_TILES, HEAD]), op=ALU.mult,
+            )
+            sin_gain = const.tile([P, TOKEN_TILES, HEAD], F32, name="sin_gain_" + name)
+            nc.gpsimd.tensor_tensor(
+                out=sin_gain[:], in0=sin_sb[:],
+                in1=swapped[:].unsqueeze(1).to_broadcast([P, TOKEN_TILES, HEAD]), op=ALU.mult,
+            )
+            return cos_gain, sin_gain
+
+        tables_q = rope_tables(gain_q, "q")
+        tables_k = rope_tables(gain_k, "k")
+
+        h_codes = const.tile([P, TOKEN_TILES, PASSES, P], U32, align_bytes=64)
+        h_scales = const.tile([P, TOKEN_TILES, PASSES, P], U8, align_bytes=64)
+        x_ss = const.tile([P, TOKEN_TILES], F32)
+        x_rms = const.tile([P, TOKEN_TILES], F32)
+        x_rstd = const.tile([P, TOKEN_TILES], F32)
+        lnw_pairs = lnw[:].rearrange("p (c j e) -> p c j e", j=P, e=2)
+
+        h_perm = {}
+        grouped_h = {}
+
+        def x_stats(i):
+            nc.scalar.activation(
+                out=squares[:], in_=x_sb[:, i, :], func=ACT.Square, accum_out=x_ss[:, i : i + 1]
+            )
+            nc.scalar.activation(
+                out=x_rms[:, i : i + 1], in_=x_ss[:, i : i + 1], func=ACT.Sqrt,
+                scale=1.0 / HID, bias=eps[:, 0:1],
+            )
+
+        def x_scale(i):
+            nc.vector.reciprocal(out=x_rstd[:, i : i + 1], in_=x_rms[:, i : i + 1])
+            h_tile = hpool.tile([P, 2 * PASSES, 2, P], BF16)
+            x_pairs = x_sb[:, i, :].rearrange("p (c j e) -> p c j e", j=P, e=2)
+            for e in range(2):
+                nc.vector.scalar_tensor_tensor(
+                    out=h_tile[:, :, e, :], in0=x_pairs[:, :, :, e], scalar=x_rstd[:, i : i + 1],
+                    in1=lnw_pairs[:, :, :, e], op0=ALU.mult, op1=ALU.mult,
+                )
+            h_perm[i] = h_tile
+
+        def x_transpose(i):
+            grouped = hpool.tile([P, PASSES, P, PACK], BF16, align_bytes=64)
+            for half in range(2):
+                h_t = tp_psum.tile([P, 2 * PACK, P], BF16, tag="tp")
+                for b in range(2 * PACK):
+                    c, e = divmod(half * 2 * PACK + b, 2)
+                    nc.tensor.transpose(h_t[:, b, :], h_perm[i][:, c, e, :], ident_bf[:])
+                dst = grouped[:, 2 * half : 2 * half + 2, :, :]
+                src = h_t[:].rearrange("p (g t) r -> p g r t", t=PACK)
+                if half == 0:
+                    nc.scalar.copy(out=dst, in_=src)
+                else:
+                    nc.vector.tensor_copy(out=dst, in_=src)
+            grouped_h[i] = grouped
+
+        def x_quantise(i):
+            nc.vector.quantize_mx(
+                out=h_codes[:, i, :, :].rearrange("p g r -> p (g r)").bitcast(FP8X4),
+                scales=h_scales[:, i, :, :].rearrange("p g r -> p (g r)"),
+                in_=grouped_h[i][:].rearrange("p g r t -> p (g r t)"),
+            )
+
+        x_stats(0)
+        x_stats(1)
+        x_scale(0)
+        for i in range(TOKEN_TILES):
+            if i + 2 < TOKEN_TILES:
+                x_stats(i + 2)
+            if i + 1 < TOKEN_TILES:
+                x_scale(i + 1)
+            x_transpose(i)
+            x_quantise(i)
+
+        grouped_w = {}
+        w_codes = {}
+        w_scales = {}
+        acc = {}
+        u_sb = {}
+        rot = {}
+        rms_sb = {}
+        rstd = {}
+
+        def transpose_weights(n, vector_helps):
+            for g in range(PASSES):
+                grouped = gpool.tile([P, GROUP * PACK], BF16, align_bytes=64)
+                grouped_words = grouped[:].bitcast(F32).rearrange("p (n u) -> p n u", u=2)
+                for rp in range(2):
+                    w_t = tp_psum.tile([P, 2, 2 * P], F32, tag="tp")
+                    for u in range(2):
+                        for rr in range(2):
+                            first = (K_PASS // 2) * g + P * u
+                            nc.tensor.transpose(
+                                w_t[:, u, rr * P : (rr + 1) * P],
+                                w_sb[n][:, 2 * rp + rr, :].bitcast(F32)[:, first : first + P],
+                                ident_f[:],
+                            )
+                    dst = grouped_words[:, rp * 2 * P : (rp + 1) * 2 * P, :]
+                    src = w_t[:].rearrange("p u n -> p n u")
+                    if vector_helps and rp == 1:
+                        nc.vector.tensor_copy(out=dst, in_=src)
+                    else:
+                        nc.scalar.copy(out=dst, in_=src)
+                grouped_w[(n, g)] = grouped
+            if n + WEIGHT_BUFS < GROUPS:
+                load_weights(n + WEIGHT_BUFS)
+
+        def quantise_weights(n):
+            codes = cpool.tile([P, PASSES, GROUP], U32, align_bytes=64)
+            scales = cpool.tile([P, PASSES, GROUP], U8, align_bytes=64)
+            for g in range(PASSES):
+                nc.vector.quantize_mx(
+                    out=codes[:, g, :].bitcast(FP8X4), scales=scales[:, g, :], in_=grouped_w[(n, g)][:]
+                )
+            w_codes[n] = codes
+            w_scales[n] = scales
+
+        def project(n):
+            for i in range(TOKEN_TILES):
+                bank = acc_psum.tile([P, GROUP], F32, tag="acc")
+                for g in range(PASSES):
+                    nc.tensor.matmul_mx(
+                        out=bank[:],
+                        lhsT=h_codes[:, i, g, :].bitcast(FP8X4),
+                        lhsT_scale=h_scales[:, i, g, :],
+                        rhs=w_codes[n][:, g, :].bitcast(FP8X4),
+                        rhs_scale=w_scales[n][:, g, :],
+                        start=(g == 0),
+                        stop=(g == PASSES - 1),
+                    )
+                acc[(n, i)] = bank
+
+        def add_bias(n):
+            u = epool.tile([P, TOKEN_TILES, GROUP_HEADS, HEAD], F32)
+            for i in range(TOKEN_TILES):
+                nc.vector.tensor_tensor(
+                    out=u[:, i, :, :].rearrange("p h d -> p (h d)"), in0=acc[(n, i)][:],
+                    in1=bias[:, n * GROUP : (n + 1) * GROUP], op=ALU.add,
+                )
+            u_sb[n] = u
+
+        def sum_squares(n):
+            ss = stats.tile([P, TOKEN_TILES * GROUP_HEADS], F32)
+            for i in range(TOKEN_TILES):
+                for h in range(GROUP_HEADS):
+                    col = i * GROUP_HEADS + h
+                    nc.scalar.activation(
+                        out=squares[:, col * HEAD : (col + 1) * HEAD], in_=u_sb[n][:, i, h, :], func=ACT.Square,
+                        accum_out=ss[:, col : col + 1],
+                    )
+            rms = stats.tile([P, TOKEN_TILES * GROUP_HEADS], F32)
+            nc.scalar.activation(out=rms[:], in_=ss[:], func=ACT.Sqrt, scale=1.0 / HEAD, bias=eps[:, 0:1])
+            rms_sb[n] = rms
+
+        def invert(n):
+            inv = stats.tile([P, TOKEN_TILES * GROUP_HEADS], F32)
+            nc.vector.reciprocal(out=inv[:], in_=rms_sb[n][:])
+            rstd[n] = inv
+
+        def rotate(n, tables):
+            cos_gain, sin_gain = tables
+            u = u_sb[n]
+            shape = [P, TOKEN_TILES, GROUP_HEADS, HEAD]
+            half_shape = [P, TOKEN_TILES, GROUP_HEADS, HALF]
+            straight = epool.tile(shape, F32)
+            nc.vector.tensor_tensor(
+                out=straight[:], in0=u[:], in1=cos_gain[:].unsqueeze(2).to_broadcast(shape), op=ALU.mult
+            )
+            crossed = scratch.tile(shape, F32)
+            nc.vector.tensor_tensor(
+                out=crossed[:, :, :, 0:HALF], in0=u[:, :, :, HALF:HEAD],
+                in1=sin_gain[:, :, 0:HALF].unsqueeze(2).to_broadcast(half_shape), op=ALU.mult,
+            )
+            nc.vector.tensor_tensor(
+                out=crossed[:, :, :, HALF:HEAD], in0=u[:, :, :, 0:HALF],
+                in1=sin_gain[:, :, HALF:HEAD].unsqueeze(2).to_broadcast(half_shape), op=ALU.mult,
+            )
+            nc.vector.tensor_tensor(out=straight[:], in0=straight[:], in1=crossed[:], op=ALU.add)
+            rot[n] = straight
+
+        def scale_and_store(n):
+            for i in range(TOKEN_TILES):
+                for h in range(GROUP_HEADS):
+                    col = i * GROUP_HEADS + h
+                    nc.scalar.activation(
+                        out=rot[n][:, i, h, :], in_=rot[n][:, i, h, :], func=ACT.Copy,
+                        scale=rstd[n][:, col : col + 1],
+                    )
+                nc.sync.dma_start(
+                    out=out_cols[n][i * P : (i + 1) * P, :],
+                    in_=rot[n][:, i, :, :].rearrange("p h d -> p (h d)"),
+                )
+
+        def store_plain(n):
+            for i in range(TOKEN_TILES):
+                nc.sync.dma_start(
+                    out=out_cols[n][i * P : (i + 1) * P, :],
+                    in_=u_sb[n][:, i, :, :].rearrange("p h d -> p (h d)"),
+                )
+
+        transpose_weights(0, True)
+        quantise_weights(0)
+        project(0)
+        transpose_weights(1, True)
+        for n in range(GROUPS):
+            if n + 2 < GROUPS:
+                transpose_weights(n + 2, False)
+            add_bias(n)
+            if n + 1 < GROUPS:
+                quantise_weights(n + 1)
+                project(n + 1)
+            if n == V_GROUP:
+                store_plain(n)
+            else:
+                sum_squares(n)
+            if n >= 1:
+                scale_and_store(n - 1)
+            if n != V_GROUP:
+                rotate(n, tables_k if n == K_GROUP else tables_q)
+                invert(n)

@@ -53,7 +53,7 @@ def tile_qwen2decoderlayer_pa_kernel(
         gpool = ctx.enter_context(tc.tile_pool(name="gpool", bufs=6))
         cpool = ctx.enter_context(tc.tile_pool(name="cpool", bufs=2))
         epool = ctx.enter_context(tc.tile_pool(name="epool", bufs=2))
-        scratch = ctx.enter_context(tc.tile_pool(name="scratch", bufs=1))
+        scratch = ctx.enter_context(tc.tile_pool(name="scratch", bufs=2))
         stats = ctx.enter_context(tc.tile_pool(name="stats", bufs=2))
         acc_psum = ctx.enter_context(tc.psum_pool(name="acc_psum", bufs=4))
         tp_psum = ctx.enter_context(tc.psum_pool(name="tp_psum", bufs=4))
@@ -294,7 +294,10 @@ def tile_qwen2decoderlayer_pa_kernel(
                 out=crossed[:, :, :, HALF:HEAD], in0=u[:, :, :, 0:HALF],
                 in1=sin_gain[:, :, HALF:HEAD].unsqueeze(2).to_broadcast(half_shape), op=ALU.mult,
             )
-            nc.vector.tensor_tensor(out=straight[:], in0=straight[:], in1=crossed[:], op=ALU.add)
+            for i in range(TOKEN_TILES):
+                nc.gpsimd.tensor_tensor(
+                    out=straight[:, i, :, :], in0=straight[:, i, :, :], in1=crossed[:, i, :, :], op=ALU.add
+                )
             rot[n] = straight
 
         def scale_and_store(n):

@@ -30,6 +30,7 @@ K_GROUP = 4
 V_GROUP = 5
 GROUPS = 6
 WEIGHT_BUFS = 4
+PSUM_BANKS = 8
 
 FLOPS = 2 * TOKENS * HID * GROUPS * GROUP
 
@@ -47,16 +48,15 @@ def tile_qwen2decoderlayer_pa_kernel(
     ]
 
     with ExitStack() as ctx:
+        ctx.enter_context(tc.manual_schedule())
         const = ctx.enter_context(tc.tile_pool(name="const", bufs=1))
         hpool = ctx.enter_context(tc.tile_pool(name="hpool", bufs=2))
         wpool = ctx.enter_context(tc.tile_pool(name="wpool", bufs=WEIGHT_BUFS))
-        gpool = ctx.enter_context(tc.tile_pool(name="gpool", bufs=6))
+        gpool = ctx.enter_context(tc.tile_pool(name="gpool", bufs=8))
         cpool = ctx.enter_context(tc.tile_pool(name="cpool", bufs=2))
         epool = ctx.enter_context(tc.tile_pool(name="epool", bufs=2))
-        scratch = ctx.enter_context(tc.tile_pool(name="scratch", bufs=2))
         stats = ctx.enter_context(tc.tile_pool(name="stats", bufs=2))
-        acc_psum = ctx.enter_context(tc.psum_pool(name="acc_psum", bufs=4))
-        tp_psum = ctx.enter_context(tc.psum_pool(name="tp_psum", bufs=4))
+        banks = ctx.enter_context(tc.psum_pool(name="banks", bufs=PSUM_BANKS))
 
         x_sb = const.tile([P, TOKEN_TILES, HID], BF16)
         lnw = const.tile([P, HID], BF16)
@@ -136,6 +136,7 @@ def tile_qwen2decoderlayer_pa_kernel(
         lnw_pairs = lnw[:].rearrange("p (c j e) -> p c j e", j=P, e=2)
 
         h_perm = {}
+        h_banks = {}
         grouped_h = {}
 
         def x_stats(i):
@@ -159,38 +160,31 @@ def tile_qwen2decoderlayer_pa_kernel(
             h_perm[i] = h_tile
 
         def x_transpose(i):
-            grouped = hpool.tile([P, PASSES, P, PACK], BF16, align_bytes=64)
             for half in range(2):
-                h_t = tp_psum.tile([P, 2 * PACK, P], BF16, tag="tp")
+                h_t = banks.tile([P, 2 * PACK, P], BF16, tag="bank")
                 for b in range(2 * PACK):
                     c, e = divmod(half * 2 * PACK + b, 2)
                     nc.tensor.transpose(h_t[:, b, :], h_perm[i][:, c, e, :], ident_bf[:])
-                dst = grouped[:, 2 * half : 2 * half + 2, :, :]
-                src = h_t[:].rearrange("p (g t) r -> p g r t", t=PACK)
-                if half == 0:
-                    nc.scalar.copy(out=dst, in_=src)
-                else:
-                    nc.vector.tensor_copy(out=dst, in_=src)
+                h_banks[(i, half)] = h_t
+
+        def x_copy_out(i):
+            grouped = gpool.tile([P, GROUP * PACK], BF16, align_bytes=64, tag="grouped")
+            grouped_view = grouped[:].rearrange("p (g r t) -> p g r t", g=PASSES, t=PACK)
+            for half in range(2):
+                nc.scalar.copy(
+                    out=grouped_view[:, 2 * half : 2 * half + 2, :, :],
+                    in_=h_banks[(i, half)][:].rearrange("p (g t) r -> p g r t", t=PACK),
+                )
             grouped_h[i] = grouped
 
         def x_quantise(i):
             nc.vector.quantize_mx(
                 out=h_codes[:, i, :, :].rearrange("p g r -> p (g r)").bitcast(FP8X4),
                 scales=h_scales[:, i, :, :].rearrange("p g r -> p (g r)"),
-                in_=grouped_h[i][:].rearrange("p g r t -> p (g r t)"),
+                in_=grouped_h[i][:],
             )
 
-        x_stats(0)
-        x_stats(1)
-        x_scale(0)
-        for i in range(TOKEN_TILES):
-            if i + 2 < TOKEN_TILES:
-                x_stats(i + 2)
-            if i + 1 < TOKEN_TILES:
-                x_scale(i + 1)
-            x_transpose(i)
-            x_quantise(i)
-
+        w_banks = {}
         grouped_w = {}
         w_codes = {}
         w_scales = {}
@@ -200,12 +194,10 @@ def tile_qwen2decoderlayer_pa_kernel(
         rms_sb = {}
         rstd = {}
 
-        def transpose_weights(n, vector_helps):
+        def transpose_weights(n):
             for g in range(PASSES):
-                grouped = gpool.tile([P, GROUP * PACK], BF16, align_bytes=64)
-                grouped_words = grouped[:].bitcast(F32).rearrange("p (n u) -> p n u", u=2)
                 for rp in range(2):
-                    w_t = tp_psum.tile([P, 2, 2 * P], F32, tag="tp")
+                    w_t = banks.tile([P, 2, 2 * P], F32, tag="bank")
                     for u in range(2):
                         for rr in range(2):
                             first = (K_PASS // 2) * g + P * u
@@ -214,29 +206,34 @@ def tile_qwen2decoderlayer_pa_kernel(
                                 w_sb[n][:, 2 * rp + rr, :].bitcast(F32)[:, first : first + P],
                                 ident_f[:],
                             )
-                    dst = grouped_words[:, rp * 2 * P : (rp + 1) * 2 * P, :]
-                    src = w_t[:].rearrange("p u n -> p n u")
-                    if vector_helps and rp == 1:
-                        nc.vector.tensor_copy(out=dst, in_=src)
-                    else:
-                        nc.scalar.copy(out=dst, in_=src)
-                grouped_w[(n, g)] = grouped
+                    w_banks[(n, g, rp)] = w_t
             if n + WEIGHT_BUFS < GROUPS:
                 load_weights(n + WEIGHT_BUFS)
 
-        def quantise_weights(n):
-            codes = cpool.tile([P, PASSES, GROUP], U32, align_bytes=64)
-            scales = cpool.tile([P, PASSES, GROUP], U8, align_bytes=64)
-            for g in range(PASSES):
-                nc.vector.quantize_mx(
-                    out=codes[:, g, :].bitcast(FP8X4), scales=scales[:, g, :], in_=grouped_w[(n, g)][:]
+        def copy_out_weights(n, g, copy):
+            grouped = gpool.tile([P, GROUP * PACK], BF16, align_bytes=64, tag="grouped")
+            grouped_words = grouped[:].bitcast(F32).rearrange("p (n u) -> p n u", u=2)
+            for rp in range(2):
+                copy(
+                    out=grouped_words[:, rp * 2 * P : (rp + 1) * 2 * P, :],
+                    in_=w_banks[(n, g, rp)][:].rearrange("p u n -> p n u"),
                 )
-            w_codes[n] = codes
-            w_scales[n] = scales
+            grouped_w[(n, g)] = grouped
+
+        def quantise_weights(n, g):
+            if g == 0:
+                codes = cpool.tile([P, PASSES, GROUP], U32, align_bytes=64)
+                scales = cpool.tile([P, PASSES, GROUP], U8, align_bytes=64)
+                w_codes[n] = codes
+                w_scales[n] = scales
+            nc.vector.quantize_mx(
+                out=w_codes[n][:, g, :].bitcast(FP8X4), scales=w_scales[n][:, g, :],
+                in_=grouped_w[(n, g)][:],
+            )
 
         def project(n):
             for i in range(TOKEN_TILES):
-                bank = acc_psum.tile([P, GROUP], F32, tag="acc")
+                bank = banks.tile([P, GROUP], F32, tag="bank")
                 for g in range(PASSES):
                     nc.tensor.matmul_mx(
                         out=bank[:],
@@ -249,14 +246,14 @@ def tile_qwen2decoderlayer_pa_kernel(
                     )
                 acc[(n, i)] = bank
 
-        def add_bias(n):
-            u = epool.tile([P, TOKEN_TILES, GROUP_HEADS, HEAD], F32)
-            for i in range(TOKEN_TILES):
-                nc.vector.tensor_tensor(
-                    out=u[:, i, :, :].rearrange("p h d -> p (h d)"), in0=acc[(n, i)][:],
-                    in1=bias[:, n * GROUP : (n + 1) * GROUP], op=ALU.add,
-                )
-            u_sb[n] = u
+        def add_bias(n, i):
+            if i == 0:
+                u = epool.tile([P, TOKEN_TILES, GROUP_HEADS, HEAD], F32)
+                u_sb[n] = u
+            nc.vector.tensor_tensor(
+                out=u_sb[n][:, i, :, :].rearrange("p h d -> p (h d)"), in0=acc[(n, i)][:],
+                in1=bias[:, n * GROUP : (n + 1) * GROUP], op=ALU.add,
+            )
 
         def sum_squares(n):
             ss = stats.tile([P, TOKEN_TILES * GROUP_HEADS], F32)
@@ -264,8 +261,8 @@ def tile_qwen2decoderlayer_pa_kernel(
                 for h in range(GROUP_HEADS):
                     col = i * GROUP_HEADS + h
                     nc.scalar.activation(
-                        out=squares[:, col * HEAD : (col + 1) * HEAD], in_=u_sb[n][:, i, h, :], func=ACT.Square,
-                        accum_out=ss[:, col : col + 1],
+                        out=squares[:, col * HEAD : (col + 1) * HEAD], in_=u_sb[n][:, i, h, :],
+                        func=ACT.Square, accum_out=ss[:, col : col + 1],
                     )
             rms = stats.tile([P, TOKEN_TILES * GROUP_HEADS], F32)
             nc.scalar.activation(out=rms[:], in_=ss[:], func=ACT.Sqrt, scale=1.0 / HEAD, bias=eps[:, 0:1])
@@ -285,7 +282,7 @@ def tile_qwen2decoderlayer_pa_kernel(
             nc.vector.tensor_tensor(
                 out=straight[:], in0=u[:], in1=cos_gain[:].unsqueeze(2).to_broadcast(shape), op=ALU.mult
             )
-            crossed = scratch.tile(shape, F32)
+            crossed = epool.tile(shape, F32)
             nc.vector.tensor_tensor(
                 out=crossed[:, :, :, 0:HALF], in0=u[:, :, :, HALF:HEAD],
                 in1=sin_gain[:, :, 0:HALF].unsqueeze(2).to_broadcast(half_shape), op=ALU.mult,
@@ -320,23 +317,45 @@ def tile_qwen2decoderlayer_pa_kernel(
                     in_=u_sb[n][:, i, :, :].rearrange("p h d -> p (h d)"),
                 )
 
-        transpose_weights(0, True)
-        quantise_weights(0)
+        for i in range(TOKEN_TILES):
+            x_stats(i)
+        for i in range(TOKEN_TILES):
+            x_scale(i)
+            x_transpose(i)
+        for i in range(TOKEN_TILES):
+            x_copy_out(i)
+        transpose_weights(0)
+        for g in range(PASSES):
+            copy_out_weights(0, g, nc.vector.tensor_copy)
+            x_quantise(g)
+        for g in range(PASSES):
+            quantise_weights(0, g)
+        transpose_weights(1)
+        for g in range(PASSES // 2):
+            copy_out_weights(1, g, nc.scalar.copy)
         project(0)
-        transpose_weights(1, True)
+        for g in range(PASSES // 2, PASSES):
+            copy_out_weights(1, g, nc.scalar.copy)
+
         for n in range(GROUPS):
+            for j in range(TOKEN_TILES):
+                add_bias(n, j)
+                if n + 1 < GROUPS:
+                    quantise_weights(n + 1, j)
+            if n >= 1:
+                invert(n - 1)
             if n + 2 < GROUPS:
-                transpose_weights(n + 2, False)
-            add_bias(n)
-            if n + 1 < GROUPS:
-                quantise_weights(n + 1)
-                project(n + 1)
+                transpose_weights(n + 2)
             if n == V_GROUP:
                 store_plain(n)
             else:
                 sum_squares(n)
+            if n + 2 < GROUPS:
+                for g in range(PASSES):
+                    copy_out_weights(n + 2, g, nc.scalar.copy)
+            if n + 1 < GROUPS:
+                project(n + 1)
             if n >= 1:
                 scale_and_store(n - 1)
             if n != V_GROUP:
                 rotate(n, tables_k if n == K_GROUP else tables_q)
-                invert(n)

@@ -30,7 +30,8 @@ K_GROUP = 4
 V_GROUP = 5
 GROUPS = 6
 WEIGHT_BUFS = 4
-PSUM_BANKS = 8
+RING_BANKS = 6
+RUN_AHEAD = 3
 
 FLOPS = 2 * TOKENS * HID * GROUPS * GROUP
 
@@ -56,7 +57,8 @@ def tile_qwen2decoderlayer_pa_kernel(
         cpool = ctx.enter_context(tc.tile_pool(name="cpool", bufs=2))
         epool = ctx.enter_context(tc.tile_pool(name="epool", bufs=2))
         stats = ctx.enter_context(tc.tile_pool(name="stats", bufs=2))
-        banks = ctx.enter_context(tc.psum_pool(name="banks", bufs=PSUM_BANKS))
+        banks = ctx.enter_context(tc.psum_pool(name="banks", bufs=RING_BANKS))
+        rope_psum = ctx.enter_context(tc.psum_pool(name="rope_psum", bufs=1))
 
         x_sb = const.tile([P, TOKEN_TILES, HID], BF16)
         lnw = const.tile([P, HID], BF16)
@@ -128,6 +130,17 @@ def tile_qwen2decoderlayer_pa_kernel(
         tables_q = rope_tables(gain_q, "q")
         tables_k = rope_tables(gain_k, "k")
 
+        def tables_to_psum(tables):
+            in_psum = []
+            for table, tag in zip(tables, ("cos", "sin")):
+                bank = rope_psum.tile([P, TOKEN_TILES, HEAD], F32, tag=tag, name="rope_" + tag)
+                nc.tensor.matmul(
+                    out=bank[:].rearrange("p i d -> p (i d)"), lhsT=ident_f[:],
+                    rhs=table[:].rearrange("p i d -> p (i d)"), start=True, stop=True,
+                )
+                in_psum.append(bank)
+            return in_psum
+
         h_codes = const.tile([P, TOKEN_TILES, PASSES, P], U32, align_bytes=64)
         h_scales = const.tile([P, TOKEN_TILES, PASSES, P], U8, align_bytes=64)
         x_ss = const.tile([P, TOKEN_TILES], F32)
@@ -194,20 +207,19 @@ def tile_qwen2decoderlayer_pa_kernel(
         rms_sb = {}
         rstd = {}
 
-        def transpose_weights(n):
-            for g in range(PASSES):
-                for rp in range(2):
-                    w_t = banks.tile([P, 2, 2 * P], F32, tag="bank")
-                    for u in range(2):
-                        for rr in range(2):
-                            first = (K_PASS // 2) * g + P * u
-                            nc.tensor.transpose(
-                                w_t[:, u, rr * P : (rr + 1) * P],
-                                w_sb[n][:, 2 * rp + rr, :].bitcast(F32)[:, first : first + P],
-                                ident_f[:],
-                            )
-                    w_banks[(n, g, rp)] = w_t
-            if n + WEIGHT_BUFS < GROUPS:
+        def transpose_weights(n, g):
+            for rp in range(2):
+                w_t = banks.tile([P, 2, 2 * P], F32, tag="bank")
+                for u in range(2):
+                    for rr in range(2):
+                        first = (K_PASS // 2) * g + P * u
+                        nc.tensor.transpose(
+                            w_t[:, u, rr * P : (rr + 1) * P],
+                            w_sb[n][:, 2 * rp + rr, :].bitcast(F32)[:, first : first + P],
+                            ident_f[:],
+                        )
+                w_banks[(n, g, rp)] = w_t
+            if g == PASSES - 1 and n + WEIGHT_BUFS < GROUPS:
                 load_weights(n + WEIGHT_BUFS)
 
         def copy_out_weights(n, g, copy):
@@ -320,32 +332,43 @@ def tile_qwen2decoderlayer_pa_kernel(
         for i in range(TOKEN_TILES):
             x_stats(i)
         for i in range(TOKEN_TILES):
+            if i >= RUN_AHEAD:
+                x_copy_out(i - RUN_AHEAD)
             x_scale(i)
             x_transpose(i)
-        for i in range(TOKEN_TILES):
+        for i in range(TOKEN_TILES - RUN_AHEAD, TOKEN_TILES):
             x_copy_out(i)
-        transpose_weights(0)
+
+        for g in range(RUN_AHEAD):
+            transpose_weights(0, g)
         for g in range(PASSES):
             copy_out_weights(0, g, nc.vector.tensor_copy)
+            if g + RUN_AHEAD < PASSES:
+                transpose_weights(0, g + RUN_AHEAD)
             x_quantise(g)
         for g in range(PASSES):
             quantise_weights(0, g)
-        transpose_weights(1)
-        for g in range(PASSES // 2):
+
+        for g in range(RUN_AHEAD):
+            transpose_weights(1, g)
+        for g in range(PASSES):
             copy_out_weights(1, g, nc.scalar.copy)
+            if g + RUN_AHEAD < PASSES:
+                transpose_weights(1, g + RUN_AHEAD)
         project(0)
-        for g in range(PASSES // 2, PASSES):
-            copy_out_weights(1, g, nc.scalar.copy)
+        rope = tables_to_psum(tables_q)
 
         for n in range(GROUPS):
-            for j in range(TOKEN_TILES):
-                add_bias(n, j)
-                if n + 1 < GROUPS:
-                    quantise_weights(n + 1, j)
+            if n + 1 < GROUPS:
+                for g in range(PASSES):
+                    quantise_weights(n + 1, g)
+            for i in range(TOKEN_TILES):
+                add_bias(n, i)
             if n >= 1:
                 invert(n - 1)
             if n + 2 < GROUPS:
-                transpose_weights(n + 2)
+                for g in range(RUN_AHEAD):
+                    transpose_weights(n + 2, g)
             if n == V_GROUP:
                 store_plain(n)
             else:
@@ -353,9 +376,13 @@ def tile_qwen2decoderlayer_pa_kernel(
             if n + 2 < GROUPS:
                 for g in range(PASSES):
                     copy_out_weights(n + 2, g, nc.scalar.copy)
+                    if g + RUN_AHEAD < PASSES:
+                        transpose_weights(n + 2, g + RUN_AHEAD)
             if n + 1 < GROUPS:
                 project(n + 1)
             if n >= 1:
                 scale_and_store(n - 1)
             if n != V_GROUP:
-                rotate(n, tables_k if n == K_GROUP else tables_q)
+                rotate(n, rope)
+            if n + 1 == K_GROUP:
+                rope = tables_to_psum(tables_k)

@@ -53,7 +53,7 @@ def tile_qwen2decoderlayer_pa_kernel(
         const = ctx.enter_context(tc.tile_pool(name="const", bufs=1))
         hpool = ctx.enter_context(tc.tile_pool(name="hpool", bufs=2))
         wpool = ctx.enter_context(tc.tile_pool(name="wpool", bufs=WEIGHT_BUFS))
-        gpool = ctx.enter_context(tc.tile_pool(name="gpool", bufs=8))
+        gpool = ctx.enter_context(tc.tile_pool(name="gpool", bufs=6))
         cpool = ctx.enter_context(tc.tile_pool(name="cpool", bufs=2))
         epool = ctx.enter_context(tc.tile_pool(name="epool", bufs=2))
         stats = ctx.enter_context(tc.tile_pool(name="stats", bufs=2))
@@ -222,10 +222,10 @@ def tile_qwen2decoderlayer_pa_kernel(
             if g == PASSES - 1 and n + WEIGHT_BUFS < GROUPS:
                 load_weights(n + WEIGHT_BUFS)
 
-        def copy_out_weights(n, g, copy):
+        def copy_out_weights(n, g, copies):
             grouped = gpool.tile([P, GROUP * PACK], BF16, align_bytes=64, tag="grouped")
             grouped_words = grouped[:].bitcast(F32).rearrange("p (n u) -> p n u", u=2)
-            for rp in range(2):
+            for rp, copy in enumerate(copies):
                 copy(
                     out=grouped_words[:, rp * 2 * P : (rp + 1) * 2 * P, :],
                     in_=w_banks[(n, g, rp)][:].rearrange("p u n -> p n u"),
@@ -290,7 +290,7 @@ def tile_qwen2decoderlayer_pa_kernel(
             u = u_sb[n]
             shape = [P, TOKEN_TILES, GROUP_HEADS, HEAD]
             half_shape = [P, TOKEN_TILES, GROUP_HEADS, HALF]
-            straight = epool.tile(shape, F32)
+            straight = epool.tile(shape, F32, bufs=3)
             nc.vector.tensor_tensor(
                 out=straight[:], in0=u[:], in1=cos_gain[:].unsqueeze(2).to_broadcast(shape), op=ALU.mult
             )
@@ -342,7 +342,7 @@ def tile_qwen2decoderlayer_pa_kernel(
         for g in range(RUN_AHEAD):
             transpose_weights(0, g)
         for g in range(PASSES):
-            copy_out_weights(0, g, nc.vector.tensor_copy)
+            copy_out_weights(0, g, (nc.scalar.copy, nc.vector.tensor_copy))
             if g + RUN_AHEAD < PASSES:
                 transpose_weights(0, g + RUN_AHEAD)
             x_quantise(g)
@@ -352,7 +352,7 @@ def tile_qwen2decoderlayer_pa_kernel(
         for g in range(RUN_AHEAD):
             transpose_weights(1, g)
         for g in range(PASSES):
-            copy_out_weights(1, g, nc.scalar.copy)
+            copy_out_weights(1, g, (nc.scalar.copy, nc.scalar.copy))
             if g + RUN_AHEAD < PASSES:
                 transpose_weights(1, g + RUN_AHEAD)
         project(0)
@@ -375,7 +375,8 @@ def tile_qwen2decoderlayer_pa_kernel(
                 sum_squares(n)
             if n + 2 < GROUPS:
                 for g in range(PASSES):
-                    copy_out_weights(n + 2, g, nc.scalar.copy)
+                    first_copy = nc.vector.tensor_copy if g == 0 else nc.scalar.copy
+                    copy_out_weights(n + 2, g, (first_copy, nc.scalar.copy))
                     if g + RUN_AHEAD < PASSES:
                         transpose_weights(n + 2, g + RUN_AHEAD)
             if n + 1 < GROUPS:

@@ -7,6 +7,7 @@ F32 = mybir.dt.float32
 BF16 = mybir.dt.bfloat16
 U32 = mybir.dt.uint32
 U8 = mybir.dt.uint8
+I32 = mybir.dt.int32
 FP8X4 = mybir.dt.float8_e4m3fn_x4
 ACT = mybir.ActivationFunctionType
 ALU = mybir.AluOpType
@@ -42,6 +43,7 @@ def tile_qwen2decoderlayer_pa_kernel(
     nc = tc.nc
 
     weight_rows = [wq[n * GROUP : (n + 1) * GROUP, :] for n in range(Q_GROUPS)] + [wk, wv]
+    bias_rows = [bq[n * GROUP : (n + 1) * GROUP] for n in range(Q_GROUPS)] + [bk, bv]
     q_flat = out_0.rearrange("t h d -> t (h d)")
     out_cols = [q_flat[:, n * GROUP : (n + 1) * GROUP] for n in range(Q_GROUPS)] + [
         out_1.rearrange("t h d -> t (h d)"),
@@ -61,21 +63,12 @@ def tile_qwen2decoderlayer_pa_kernel(
         rope_psum = ctx.enter_context(tc.psum_pool(name="rope_psum", bufs=1))
 
         x_sb = const.tile([P, TOKEN_TILES, HID], BF16)
-        lnw = const.tile([P, HID], BF16)
         nc.sync.dma_start(out=x_sb[:, 0, :], in_=x[0:P, :])
-        nc.sync.dma_start(out=lnw[:], in_=ln1_w.partition_broadcast(P))
+        lnw_row = const.tile([P, HID], BF16)
+        nc.vector.memset(lnw_row[:].bitcast(I32), 0)
+        nc.sync.dma_start(out=lnw_row[0:1, :], in_=ln1_w.unsqueeze(0))
         for i in range(1, TOKEN_TILES):
             nc.sync.dma_start(out=x_sb[:, i, :], in_=x[i * P : (i + 1) * P, :])
-
-        w_sb = {}
-
-        def load_weights(n):
-            w_rows = wpool.tile([P, ROW_TILES, HID], BF16)
-            nc.sync.dma_start(out=w_rows[:], in_=weight_rows[n].rearrange("(r p) k -> p r k", p=P))
-            w_sb[n] = w_rows
-
-        load_weights(0)
-        load_weights(1)
         cos_sb = const.tile([P, TOKEN_TILES, HEAD], BF16)
         nc.sync.dma_start(out=cos_sb[:], in_=cos.rearrange("(i p) d -> p i d", p=P))
         sin_sb = const.tile([P, TOKEN_TILES, HEAD], BF16)
@@ -84,15 +77,19 @@ def tile_qwen2decoderlayer_pa_kernel(
         nc.sync.dma_start(out=gain_q[:], in_=q_norm_w.partition_broadcast(P))
         gain_k = const.tile([P, HEAD], BF16)
         nc.sync.dma_start(out=gain_k[:], in_=k_norm_w.partition_broadcast(P))
+
         bias = const.tile([P, GROUPS * GROUP], BF16)
-        nc.sync.dma_start(out=bias[:, 0 : Q_GROUPS * GROUP], in_=bq.partition_broadcast(P))
-        nc.sync.dma_start(
-            out=bias[:, K_GROUP * GROUP : (K_GROUP + 1) * GROUP], in_=bk.partition_broadcast(P)
-        )
-        nc.sync.dma_start(
-            out=bias[:, V_GROUP * GROUP : (V_GROUP + 1) * GROUP], in_=bv.partition_broadcast(P)
-        )
-        for n in range(2, WEIGHT_BUFS):
+        w_sb = {}
+
+        def load_weights(n):
+            w_rows = wpool.tile([P, ROW_TILES, HID], BF16)
+            nc.sync.dma_start(out=w_rows[:], in_=weight_rows[n].rearrange("(r p) k -> p r k", p=P))
+            nc.sync.dma_start(
+                out=bias[:, n * GROUP : (n + 1) * GROUP], in_=bias_rows[n].partition_broadcast(P)
+            )
+            w_sb[n] = w_rows
+
+        for n in range(WEIGHT_BUFS):
             load_weights(n)
 
         ident_bf = const.tile([P, P], BF16)
@@ -146,6 +143,15 @@ def tile_qwen2decoderlayer_pa_kernel(
         x_ss = const.tile([P, TOKEN_TILES], F32)
         x_rms = const.tile([P, TOKEN_TILES], F32)
         x_rstd = const.tile([P, TOKEN_TILES], F32)
+        ones = const.tile([P, P], BF16)
+        nc.vector.memset(ones[:], 1.0)
+        lnw = const.tile([P, HID], BF16)
+        for c in range(HID // GROUP):
+            spread = banks.tile([P, GROUP], F32, tag="bank")
+            nc.tensor.matmul(
+                out=spread[:], lhsT=ones[:], rhs=lnw_row[:, c * GROUP : (c + 1) * GROUP], start=True, stop=True
+            )
+            nc.vector.tensor_copy(out=lnw[:, c * GROUP : (c + 1) * GROUP], in_=spread[:])
         lnw_pairs = lnw[:].rearrange("p (c j e) -> p c j e", j=P, e=2)
 
         h_perm = {}

@@ -5,9 +5,9 @@ from concourse.masks import make_identity
 
 F32 = mybir.dt.float32
 BF16 = mybir.dt.bfloat16
+I32 = mybir.dt.int32
 U32 = mybir.dt.uint32
 U8 = mybir.dt.uint8
-I32 = mybir.dt.int32
 FP8X4 = mybir.dt.float8_e4m3fn_x4
 ACT = mybir.ActivationFunctionType
 ALU = mybir.AluOpType
@@ -23,6 +23,8 @@ TOKEN_TILES = TOKENS // P
 PACK = 4
 K_PASS = P * PACK
 PASSES = HID // K_PASS
+PAIR = 2
+WORDS = PACK // PAIR
 GROUP = 512
 GROUP_HEADS = GROUP // HEAD
 ROW_TILES = GROUP // P
@@ -30,9 +32,13 @@ Q_GROUPS = 4
 K_GROUP = 4
 V_GROUP = 5
 GROUPS = 6
+
 WEIGHT_BUFS = 4
 RING_BANKS = 6
-RUN_AHEAD = 3
+UNIT_BANKS = 2
+RUN_AHEAD = RING_BANKS // UNIT_BANKS
+H_BLOCKS = PACK * PASSES // UNIT_BANKS
+BANK_ROW_TILES = ROW_TILES // UNIT_BANKS
 
 FLOPS = 2 * TOKENS * HID * GROUPS * GROUP
 
@@ -59,7 +65,7 @@ def tile_qwen2decoderlayer_pa_kernel(
         cpool = ctx.enter_context(tc.tile_pool(name="cpool", bufs=2))
         epool = ctx.enter_context(tc.tile_pool(name="epool", bufs=2))
         stats = ctx.enter_context(tc.tile_pool(name="stats", bufs=2))
-        banks = ctx.enter_context(tc.psum_pool(name="banks", bufs=RING_BANKS))
+        ring = ctx.enter_context(tc.psum_pool(name="ring", bufs=RING_BANKS))
         rope_psum = ctx.enter_context(tc.psum_pool(name="rope_psum", bufs=1))
 
         x_sb = const.tile([P, TOKEN_TILES, HID], BF16)
@@ -143,18 +149,19 @@ def tile_qwen2decoderlayer_pa_kernel(
         x_ss = const.tile([P, TOKEN_TILES], F32)
         x_rms = const.tile([P, TOKEN_TILES], F32)
         x_rstd = const.tile([P, TOKEN_TILES], F32)
+
         ones = const.tile([P, P], BF16)
         nc.vector.memset(ones[:], 1.0)
         lnw = const.tile([P, HID], BF16)
         for c in range(HID // GROUP):
-            spread = banks.tile([P, GROUP], F32, tag="bank")
+            spread = ring.tile([P, GROUP], F32, tag="bank")
             nc.tensor.matmul(
                 out=spread[:], lhsT=ones[:], rhs=lnw_row[:, c * GROUP : (c + 1) * GROUP], start=True, stop=True
             )
             nc.vector.tensor_copy(out=lnw[:, c * GROUP : (c + 1) * GROUP], in_=spread[:])
-        lnw_pairs = lnw[:].rearrange("p (c j e) -> p c j e", j=P, e=2)
+        lnw_pairs = lnw[:].rearrange("p (c j e) -> p c j e", j=P, e=PAIR)
 
-        h_perm = {}
+        h_tiles = {}
         h_banks = {}
         grouped_h = {}
 
@@ -169,29 +176,30 @@ def tile_qwen2decoderlayer_pa_kernel(
 
         def x_scale(i):
             nc.vector.reciprocal(out=x_rstd[:, i : i + 1], in_=x_rms[:, i : i + 1])
-            h_tile = hpool.tile([P, 2 * PASSES, 2, P], BF16)
-            x_pairs = x_sb[:, i, :].rearrange("p (c j e) -> p c j e", j=P, e=2)
-            for e in range(2):
+            h_tile = hpool.tile([P, PAIR * PASSES, PAIR, P], BF16)
+            x_pairs = x_sb[:, i, :].rearrange("p (c j e) -> p c j e", j=P, e=PAIR)
+            for e in range(PAIR):
                 nc.vector.scalar_tensor_tensor(
                     out=h_tile[:, :, e, :], in0=x_pairs[:, :, :, e], scalar=x_rstd[:, i : i + 1],
                     in1=lnw_pairs[:, :, :, e], op0=ALU.mult, op1=ALU.mult,
                 )
-            h_perm[i] = h_tile
+            h_tiles[i] = h_tile
 
         def x_transpose(i):
-            for half in range(2):
-                h_t = banks.tile([P, 2 * PACK, P], BF16, tag="bank")
-                for b in range(2 * PACK):
-                    c, e = divmod(half * 2 * PACK + b, 2)
-                    nc.tensor.transpose(h_t[:, b, :], h_perm[i][:, c, e, :], ident_bf[:])
+            for half in range(UNIT_BANKS):
+                h_t = ring.tile([P, H_BLOCKS, P], BF16, tag="bank")
+                for b in range(H_BLOCKS):
+                    c, e = divmod(half * H_BLOCKS + b, PAIR)
+                    nc.tensor.transpose(h_t[:, b, :], h_tiles[i][:, c, e, :], ident_bf[:])
                 h_banks[(i, half)] = h_t
 
         def x_copy_out(i):
             grouped = gpool.tile([P, GROUP * PACK], BF16, align_bytes=64, tag="grouped")
             grouped_view = grouped[:].rearrange("p (g r t) -> p g r t", g=PASSES, t=PACK)
-            for half in range(2):
+            bank_passes = PASSES // UNIT_BANKS
+            for half in range(UNIT_BANKS):
                 nc.scalar.copy(
-                    out=grouped_view[:, 2 * half : 2 * half + 2, :, :],
+                    out=grouped_view[:, half * bank_passes : (half + 1) * bank_passes, :, :],
                     in_=h_banks[(i, half)][:].rearrange("p (g t) r -> p g r t", t=PACK),
                 )
             grouped_h[i] = grouped
@@ -207,21 +215,21 @@ def tile_qwen2decoderlayer_pa_kernel(
         grouped_w = {}
         w_codes = {}
         w_scales = {}
-        acc = {}
+        sums = {}
         u_sb = {}
-        rot = {}
+        rotated = {}
         rms_sb = {}
         rstd = {}
 
         def transpose_weights(n, g):
-            for rp in range(2):
-                w_t = banks.tile([P, 2, 2 * P], F32, tag="bank")
-                for u in range(2):
-                    for rr in range(2):
-                        first = (K_PASS // 2) * g + P * u
+            for rp in range(UNIT_BANKS):
+                w_t = ring.tile([P, WORDS, BANK_ROW_TILES * P], F32, tag="bank")
+                for u in range(WORDS):
+                    for rr in range(BANK_ROW_TILES):
+                        first = (K_PASS // PAIR) * g + P * u
                         nc.tensor.transpose(
                             w_t[:, u, rr * P : (rr + 1) * P],
-                            w_sb[n][:, 2 * rp + rr, :].bitcast(F32)[:, first : first + P],
+                            w_sb[n][:, BANK_ROW_TILES * rp + rr, :].bitcast(F32)[:, first : first + P],
                             ident_f[:],
                         )
                 w_banks[(n, g, rp)] = w_t
@@ -230,10 +238,11 @@ def tile_qwen2decoderlayer_pa_kernel(
 
         def copy_out_weights(n, g, copies):
             grouped = gpool.tile([P, GROUP * PACK], BF16, align_bytes=64, tag="grouped")
-            grouped_words = grouped[:].bitcast(F32).rearrange("p (n u) -> p n u", u=2)
+            grouped_words = grouped[:].bitcast(F32).rearrange("p (n u) -> p n u", u=WORDS)
+            bank_features = BANK_ROW_TILES * P
             for rp, copy in enumerate(copies):
                 copy(
-                    out=grouped_words[:, rp * 2 * P : (rp + 1) * 2 * P, :],
+                    out=grouped_words[:, rp * bank_features : (rp + 1) * bank_features, :],
                     in_=w_banks[(n, g, rp)][:].rearrange("p u n -> p n u"),
                 )
             grouped_w[(n, g)] = grouped
@@ -251,7 +260,7 @@ def tile_qwen2decoderlayer_pa_kernel(
 
         def project(n):
             for i in range(TOKEN_TILES):
-                bank = banks.tile([P, GROUP], F32, tag="bank")
+                bank = ring.tile([P, GROUP], F32, tag="bank")
                 for g in range(PASSES):
                     nc.tensor.matmul_mx(
                         out=bank[:],
@@ -262,37 +271,37 @@ def tile_qwen2decoderlayer_pa_kernel(
                         start=(g == 0),
                         stop=(g == PASSES - 1),
                     )
-                acc[(n, i)] = bank
+                sums[(n, i)] = bank
 
         def add_bias(n, i):
             if i == 0:
                 u = epool.tile([P, TOKEN_TILES, GROUP_HEADS, HEAD], F32)
                 u_sb[n] = u
             nc.vector.tensor_tensor(
-                out=u_sb[n][:, i, :, :].rearrange("p h d -> p (h d)"), in0=acc[(n, i)][:],
+                out=u_sb[n][:, i, :, :].rearrange("p h d -> p (h d)"), in0=sums[(n, i)][:],
                 in1=bias[:, n * GROUP : (n + 1) * GROUP], op=ALU.add,
             )
 
-        def sum_squares(n):
+        def head_rms(n):
             ss = stats.tile([P, TOKEN_TILES * GROUP_HEADS], F32)
             for i in range(TOKEN_TILES):
-                for h in range(GROUP_HEADS):
-                    col = i * GROUP_HEADS + h
+                for head in range(GROUP_HEADS):
+                    col = i * GROUP_HEADS + head
                     nc.scalar.activation(
-                        out=squares[:, col * HEAD : (col + 1) * HEAD], in_=u_sb[n][:, i, h, :],
+                        out=squares[:, col * HEAD : (col + 1) * HEAD], in_=u_sb[n][:, i, head, :],
                         func=ACT.Square, accum_out=ss[:, col : col + 1],
                     )
             rms = stats.tile([P, TOKEN_TILES * GROUP_HEADS], F32)
             nc.scalar.activation(out=rms[:], in_=ss[:], func=ACT.Sqrt, scale=1.0 / HEAD, bias=eps[:, 0:1])
             rms_sb[n] = rms
 
-        def invert(n):
+        def invert_rms(n):
             inv = stats.tile([P, TOKEN_TILES * GROUP_HEADS], F32)
             nc.vector.reciprocal(out=inv[:], in_=rms_sb[n][:])
             rstd[n] = inv
 
-        def rotate(n, tables):
-            cos_gain, sin_gain = tables
+        def rotate(n, rope):
+            cos_gain, sin_gain = rope
             u = u_sb[n]
             shape = [P, TOKEN_TILES, GROUP_HEADS, HEAD]
             half_shape = [P, TOKEN_TILES, GROUP_HEADS, HALF]
@@ -313,19 +322,19 @@ def tile_qwen2decoderlayer_pa_kernel(
                 nc.gpsimd.tensor_tensor(
                     out=straight[:, i, :, :], in0=straight[:, i, :, :], in1=crossed[:, i, :, :], op=ALU.add
                 )
-            rot[n] = straight
+            rotated[n] = straight
 
         def scale_and_store(n):
             for i in range(TOKEN_TILES):
-                for h in range(GROUP_HEADS):
-                    col = i * GROUP_HEADS + h
+                for head in range(GROUP_HEADS):
+                    col = i * GROUP_HEADS + head
                     nc.scalar.activation(
-                        out=rot[n][:, i, h, :], in_=rot[n][:, i, h, :], func=ACT.Copy,
+                        out=rotated[n][:, i, head, :], in_=rotated[n][:, i, head, :], func=ACT.Copy,
                         scale=rstd[n][:, col : col + 1],
                     )
                 nc.sync.dma_start(
                     out=out_cols[n][i * P : (i + 1) * P, :],
-                    in_=rot[n][:, i, :, :].rearrange("p h d -> p (h d)"),
+                    in_=rotated[n][:, i, :, :].rearrange("p h d -> p (h d)"),
                 )
 
         def store_plain(n):
@@ -345,16 +354,18 @@ def tile_qwen2decoderlayer_pa_kernel(
         for i in range(TOKEN_TILES - RUN_AHEAD, TOKEN_TILES):
             x_copy_out(i)
 
+        assert TOKEN_TILES == PASSES
         for g in range(RUN_AHEAD):
             transpose_weights(0, g)
-        for g in range(PASSES):
-            copy_out_weights(0, g, (nc.scalar.copy, nc.vector.tensor_copy))
-            if g + RUN_AHEAD < PASSES:
-                transpose_weights(0, g + RUN_AHEAD)
-            x_quantise(g)
+        for step in range(PASSES):
+            copy_out_weights(0, step, (nc.scalar.copy, nc.vector.tensor_copy))
+            if step + RUN_AHEAD < PASSES:
+                transpose_weights(0, step + RUN_AHEAD)
+            x_quantise(step)
         for g in range(PASSES):
             quantise_weights(0, g)
 
+        rope = tables_to_psum(tables_q)
         for g in range(RUN_AHEAD):
             transpose_weights(1, g)
         for g in range(PASSES):
@@ -362,7 +373,6 @@ def tile_qwen2decoderlayer_pa_kernel(
             if g + RUN_AHEAD < PASSES:
                 transpose_weights(1, g + RUN_AHEAD)
         project(0)
-        rope = tables_to_psum(tables_q)
 
         for n in range(GROUPS):
             if n + 1 < GROUPS:
@@ -371,14 +381,14 @@ def tile_qwen2decoderlayer_pa_kernel(
             for i in range(TOKEN_TILES):
                 add_bias(n, i)
             if n >= 1:
-                invert(n - 1)
+                invert_rms(n - 1)
             if n + 2 < GROUPS:
                 for g in range(RUN_AHEAD):
                     transpose_weights(n + 2, g)
             if n == V_GROUP:
                 store_plain(n)
             else:
-                sum_squares(n)
+                head_rms(n)
             if n + 2 < GROUPS:
                 for g in range(PASSES):
                     first_copy = nc.vector.tensor_copy if g == 0 else nc.scalar.copy

@@ -50,10 +50,10 @@ def tile_qwen2decoderlayer_pa_kernel(
 
     weight_rows = [wq[n * GROUP : (n + 1) * GROUP, :] for n in range(Q_GROUPS)] + [wk, wv]
     bias_rows = [bq[n * GROUP : (n + 1) * GROUP] for n in range(Q_GROUPS)] + [bk, bv]
-    q_flat = out_0.rearrange("t h d -> t (h d)")
+    q_flat = out_0.rearrange("m a d -> m (a d)")
     out_cols = [q_flat[:, n * GROUP : (n + 1) * GROUP] for n in range(Q_GROUPS)] + [
-        out_1.rearrange("t h d -> t (h d)"),
-        out_2.rearrange("t h d -> t (h d)"),
+        out_1.rearrange("m a d -> m (a d)"),
+        out_2.rearrange("m a d -> m (a d)"),
     ]
 
     with ExitStack() as ctx:
@@ -153,12 +153,11 @@ def tile_qwen2decoderlayer_pa_kernel(
         ones = const.tile([P, P], BF16)
         nc.vector.memset(ones[:], 1.0)
         lnw = const.tile([P, HID], BF16)
-        for c in range(HID // GROUP):
+        for chunk in range(HID // GROUP):
+            cols = slice(chunk * GROUP, (chunk + 1) * GROUP)
             spread = ring.tile([P, GROUP], F32, tag="bank")
-            nc.tensor.matmul(
-                out=spread[:], lhsT=ones[:], rhs=lnw_row[:, c * GROUP : (c + 1) * GROUP], start=True, stop=True
-            )
-            nc.vector.tensor_copy(out=lnw[:, c * GROUP : (c + 1) * GROUP], in_=spread[:])
+            nc.tensor.matmul(out=spread[:], lhsT=ones[:], rhs=lnw_row[:, cols], start=True, stop=True)
+            nc.vector.tensor_copy(out=lnw[:, cols], in_=spread[:])
         lnw_pairs = lnw[:].rearrange("p (c j e) -> p c j e", j=P, e=PAIR)
 
         h_tiles = {}
@@ -194,20 +193,21 @@ def tile_qwen2decoderlayer_pa_kernel(
                 h_banks[(i, half)] = h_t
 
         def x_copy_out(i):
+            copy = nc.vector.tensor_copy if i == TOKEN_TILES - 1 else nc.scalar.copy
             grouped = gpool.tile([P, GROUP * PACK], BF16, align_bytes=64, tag="grouped")
-            grouped_view = grouped[:].rearrange("p (g r t) -> p g r t", g=PASSES, t=PACK)
+            grouped_view = grouped[:].rearrange("p (g m t) -> p g m t", g=PASSES, t=PACK)
             bank_passes = PASSES // UNIT_BANKS
             for half in range(UNIT_BANKS):
-                nc.scalar.copy(
+                copy(
                     out=grouped_view[:, half * bank_passes : (half + 1) * bank_passes, :, :],
-                    in_=h_banks[(i, half)][:].rearrange("p (g t) r -> p g r t", t=PACK),
+                    in_=h_banks[(i, half)][:].rearrange("p (g t) m -> p g m t", t=PACK),
                 )
             grouped_h[i] = grouped
 
         def x_quantise(i):
             nc.vector.quantize_mx(
-                out=h_codes[:, i, :, :].rearrange("p g r -> p (g r)").bitcast(FP8X4),
-                scales=h_scales[:, i, :, :].rearrange("p g r -> p (g r)"),
+                out=h_codes[:, i, :, :].rearrange("p g m -> p (g m)").bitcast(FP8X4),
+                scales=h_scales[:, i, :, :].rearrange("p g m -> p (g m)"),
                 in_=grouped_h[i][:],
             )
 
@@ -238,12 +238,12 @@ def tile_qwen2decoderlayer_pa_kernel(
 
         def copy_out_weights(n, g, copies):
             grouped = gpool.tile([P, GROUP * PACK], BF16, align_bytes=64, tag="grouped")
-            grouped_words = grouped[:].bitcast(F32).rearrange("p (n u) -> p n u", u=WORDS)
+            grouped_words = grouped[:].bitcast(F32).rearrange("p (f u) -> p f u", u=WORDS)
             bank_features = BANK_ROW_TILES * P
             for rp, copy in enumerate(copies):
                 copy(
                     out=grouped_words[:, rp * bank_features : (rp + 1) * bank_features, :],
-                    in_=w_banks[(n, g, rp)][:].rearrange("p u n -> p n u"),
+                    in_=w_banks[(n, g, rp)][:].rearrange("p u f -> p f u"),
                 )
             grouped_w[(n, g)] = grouped
 
@@ -278,7 +278,7 @@ def tile_qwen2decoderlayer_pa_kernel(
                 u = epool.tile([P, TOKEN_TILES, GROUP_HEADS, HEAD], F32)
                 u_sb[n] = u
             nc.vector.tensor_tensor(
-                out=u_sb[n][:, i, :, :].rearrange("p h d -> p (h d)"), in0=sums[(n, i)][:],
+                out=u_sb[n][:, i, :, :].rearrange("p a d -> p (a d)"), in0=sums[(n, i)][:],
                 in1=bias[:, n * GROUP : (n + 1) * GROUP], op=ALU.add,
             )
 
@@ -334,14 +334,14 @@ def tile_qwen2decoderlayer_pa_kernel(
                     )
                 nc.sync.dma_start(
                     out=out_cols[n][i * P : (i + 1) * P, :],
-                    in_=rotated[n][:, i, :, :].rearrange("p h d -> p (h d)"),
+                    in_=rotated[n][:, i, :, :].rearrange("p a d -> p (a d)"),
                 )
 
         def store_plain(n):
             for i in range(TOKEN_TILES):
                 nc.sync.dma_start(
                     out=out_cols[n][i * P : (i + 1) * P, :],
-                    in_=u_sb[n][:, i, :, :].rearrange("p h d -> p (h d)"),
+                    in_=u_sb[n][:, i, :, :].rearrange("p a d -> p (a d)"),
                 )
 
         for i in range(TOKEN_TILES):

from contextlib import ExitStack

import concourse.mybir as mybir
from concourse.masks import make_identity

F32 = mybir.dt.float32
BF16 = mybir.dt.bfloat16
I32 = mybir.dt.int32
U32 = mybir.dt.uint32
U8 = mybir.dt.uint8
FP8X4 = mybir.dt.float8_e4m3fn_x4
ACT = mybir.ActivationFunctionType
ALU = mybir.AluOpType

P = 128
TOKENS = 512
HID = 2048
HEAD = 128
HALF = HEAD // 2
EPS = 1e-6

TOKEN_TILES = TOKENS // P
PACK = 4
K_PASS = P * PACK
PASSES = HID // K_PASS
PAIR = 2
WORDS = PACK // PAIR
GROUP = 512
GROUP_HEADS = GROUP // HEAD
ROW_TILES = GROUP // P
Q_GROUPS = 4
K_GROUP = 4
V_GROUP = 5
GROUPS = 6

WEIGHT_BUFS = 4
RING_BANKS = 6
UNIT_BANKS = 2
RUN_AHEAD = RING_BANKS // UNIT_BANKS
H_BLOCKS = PACK * PASSES // UNIT_BANKS
BANK_ROW_TILES = ROW_TILES // UNIT_BANKS

FLOPS = 2 * TOKENS * HID * GROUPS * GROUP


def tile_qwen2decoderlayer_pa_kernel(
    tc, x, cos, sin, wq, bq, wk, bk, wv, bv, q_norm_w, k_norm_w, ln1_w, out_0, out_1, out_2
):
    nc = tc.nc

    weight_rows = [wq[n * GROUP : (n + 1) * GROUP, :] for n in range(Q_GROUPS)] + [wk, wv]
    bias_rows = [bq[n * GROUP : (n + 1) * GROUP] for n in range(Q_GROUPS)] + [bk, bv]
    q_flat = out_0.rearrange("m a d -> m (a d)")
    out_cols = [q_flat[:, n * GROUP : (n + 1) * GROUP] for n in range(Q_GROUPS)] + [
        out_1.rearrange("m a d -> m (a d)"),
        out_2.rearrange("m a d -> m (a d)"),
    ]

    with ExitStack() as ctx:
        ctx.enter_context(tc.manual_schedule())
        const = ctx.enter_context(tc.tile_pool(name="const", bufs=1))
        hpool = ctx.enter_context(tc.tile_pool(name="hpool", bufs=2))
        wpool = ctx.enter_context(tc.tile_pool(name="wpool", bufs=WEIGHT_BUFS))
        gpool = ctx.enter_context(tc.tile_pool(name="gpool", bufs=6))
        cpool = ctx.enter_context(tc.tile_pool(name="cpool", bufs=2))
        epool = ctx.enter_context(tc.tile_pool(name="epool", bufs=2))
        stats = ctx.enter_context(tc.tile_pool(name="stats", bufs=2))
        ring = ctx.enter_context(tc.psum_pool(name="ring", bufs=RING_BANKS))
        rope_psum = ctx.enter_context(tc.psum_pool(name="rope_psum", bufs=1))

        x_sb = const.tile([P, TOKEN_TILES, HID], BF16)
        nc.sync.dma_start(out=x_sb[:, 0, :], in_=x[0:P, :])
        lnw_row = const.tile([P, HID], BF16)
        nc.vector.memset(lnw_row[:].bitcast(I32), 0)
        nc.sync.dma_start(out=lnw_row[0:1, :], in_=ln1_w.unsqueeze(0))
        for i in range(1, TOKEN_TILES):
            nc.sync.dma_start(out=x_sb[:, i, :], in_=x[i * P : (i + 1) * P, :])
        cos_sb = const.tile([P, TOKEN_TILES, HEAD], BF16)
        nc.sync.dma_start(out=cos_sb[:], in_=cos.rearrange("(i p) d -> p i d", p=P))
        sin_sb = const.tile([P, TOKEN_TILES, HEAD], BF16)
        nc.sync.dma_start(out=sin_sb[:], in_=sin.rearrange("(i p) d -> p i d", p=P))
        gain_q = const.tile([P, HEAD], BF16)
        nc.sync.dma_start(out=gain_q[:], in_=q_norm_w.partition_broadcast(P))
        gain_k = const.tile([P, HEAD], BF16)
        nc.sync.dma_start(out=gain_k[:], in_=k_norm_w.partition_broadcast(P))

        bias = const.tile([P, GROUPS * GROUP], BF16)
        w_sb = {}

        def load_weights(n):
            w_rows = wpool.tile([P, ROW_TILES, HID], BF16)
            nc.sync.dma_start(out=w_rows[:], in_=weight_rows[n].rearrange("(r p) k -> p r k", p=P))
            nc.sync.dma_start(
                out=bias[:, n * GROUP : (n + 1) * GROUP], in_=bias_rows[n].partition_broadcast(P)
            )
            w_sb[n] = w_rows

        for n in range(WEIGHT_BUFS):
            load_weights(n)

        ident_bf = const.tile([P, P], BF16)
        make_identity(nc, ident_bf[:])
        ident_f = const.tile([P, P], F32)
        make_identity(nc, ident_f[:])
        eps = const.tile([P, 1], F32)
        nc.vector.memset(eps[:], EPS)
        warm = const.tile([P, 1], F32)
        nc.scalar.activation(out=warm[:], in_=eps[:], func=ACT.Sqrt)
        squares = const.tile([P, HID], BF16)

        def rope_tables(gain, name):
            swapped = const.tile([P, HEAD], BF16, name="swapped_" + name)
            nc.gpsimd.tensor_scalar(
                out=swapped[:, 0:HALF], in0=gain[:, HALF:HEAD], scalar1=-1.0, scalar2=0.0,
                op0=ALU.mult, op1=ALU.add,
            )
            nc.gpsimd.tensor_scalar(
                out=swapped[:, HALF:HEAD], in0=gain[:, 0:HALF], scalar1=1.0, scalar2=0.0,
                op0=ALU.mult, op1=ALU.add,
            )
            cos_gain = const.tile([P, TOKEN_TILES, HEAD], F32, name="cos_gain_" + name)
            nc.gpsimd.tensor_tensor(
                out=cos_gain[:], in0=cos_sb[:],
                in1=gain[:].unsqueeze(1).to_broadcast([P, TOKEN_TILES, HEAD]), op=ALU.mult,
            )
            sin_gain = const.tile([P, TOKEN_TILES, HEAD], F32, name="sin_gain_" + name)
            nc.gpsimd.tensor_tensor(
                out=sin_gain[:], in0=sin_sb[:],
                in1=swapped[:].unsqueeze(1).to_broadcast([P, TOKEN_TILES, HEAD]), op=ALU.mult,
            )
            return cos_gain, sin_gain

        tables_q = rope_tables(gain_q, "q")
        tables_k = rope_tables(gain_k, "k")

        def tables_to_psum(tables):
            in_psum = []
            for table, tag in zip(tables, ("cos", "sin")):
                bank = rope_psum.tile([P, TOKEN_TILES, HEAD], F32, tag=tag, name="rope_" + tag)
                nc.tensor.matmul(
                    out=bank[:].rearrange("p i d -> p (i d)"), lhsT=ident_f[:],
                    rhs=table[:].rearrange("p i d -> p (i d)"), start=True, stop=True,
                )
                in_psum.append(bank)
            return in_psum

        h_codes = const.tile([P, TOKEN_TILES, PASSES, P], U32, align_bytes=64)
        h_scales = const.tile([P, TOKEN_TILES, PASSES, P], U8, align_bytes=64)
        x_ss = const.tile([P, TOKEN_TILES], F32)
        x_rms = const.tile([P, TOKEN_TILES], F32)
        x_rstd = const.tile([P, TOKEN_TILES], F32)

        ones = const.tile([P, P], BF16)
        nc.vector.memset(ones[:], 1.0)
        lnw = const.tile([P, HID], BF16)
        for chunk in range(HID // GROUP):
            cols = slice(chunk * GROUP, (chunk + 1) * GROUP)
            spread = ring.tile([P, GROUP], F32, tag="bank")
            nc.tensor.matmul(out=spread[:], lhsT=ones[:], rhs=lnw_row[:, cols], start=True, stop=True)
            nc.vector.tensor_copy(out=lnw[:, cols], in_=spread[:])
        lnw_pairs = lnw[:].rearrange("p (c j e) -> p c j e", j=P, e=PAIR)

        h_tiles = {}
        h_banks = {}
        grouped_h = {}

        def x_stats(i):
            nc.scalar.activation(
                out=squares[:], in_=x_sb[:, i, :], func=ACT.Square, accum_out=x_ss[:, i : i + 1]
            )
            nc.scalar.activation(
                out=x_rms[:, i : i + 1], in_=x_ss[:, i : i + 1], func=ACT.Sqrt,
                scale=1.0 / HID, bias=eps[:, 0:1],
            )

        def x_scale(i):
            nc.vector.reciprocal(out=x_rstd[:, i : i + 1], in_=x_rms[:, i : i + 1])
            h_tile = hpool.tile([P, PAIR * PASSES, PAIR, P], BF16)
            x_pairs = x_sb[:, i, :].rearrange("p (c j e) -> p c j e", j=P, e=PAIR)
            for e in range(PAIR):
                nc.vector.scalar_tensor_tensor(
                    out=h_tile[:, :, e, :], in0=x_pairs[:, :, :, e], scalar=x_rstd[:, i : i + 1],
                    in1=lnw_pairs[:, :, :, e], op0=ALU.mult, op1=ALU.mult,
                )
            h_tiles[i] = h_tile

        def x_transpose(i):
            for half in range(UNIT_BANKS):
                h_t = ring.tile([P, H_BLOCKS, P], BF16, tag="bank")
                for b in range(H_BLOCKS):
                    c, e = divmod(half * H_BLOCKS + b, PAIR)
                    nc.tensor.transpose(h_t[:, b, :], h_tiles[i][:, c, e, :], ident_bf[:])
                h_banks[(i, half)] = h_t

        def x_copy_out(i):
            copy = nc.vector.tensor_copy if i == TOKEN_TILES - 1 else nc.scalar.copy
            grouped = gpool.tile([P, GROUP * PACK], BF16, align_bytes=64, tag="grouped")
            grouped_view = grouped[:].rearrange("p (g m t) -> p g m t", g=PASSES, t=PACK)
            bank_passes = PASSES // UNIT_BANKS
            for half in range(UNIT_BANKS):
                copy(
                    out=grouped_view[:, half * bank_passes : (half + 1) * bank_passes, :, :],
                    in_=h_banks[(i, half)][:].rearrange("p (g t) m -> p g m t", t=PACK),
                )
            grouped_h[i] = grouped

        def x_quantise(i):
            nc.vector.quantize_mx(
                out=h_codes[:, i, :, :].rearrange("p g m -> p (g m)").bitcast(FP8X4),
                scales=h_scales[:, i, :, :].rearrange("p g m -> p (g m)"),
                in_=grouped_h[i][:],
            )

        w_banks = {}
        grouped_w = {}
        w_codes = {}
        w_scales = {}
        sums = {}
        u_sb = {}
        rotated = {}
        rms_sb = {}
        rstd = {}

        def transpose_weights(n, g):
            for rp in range(UNIT_BANKS):
                w_t = ring.tile([P, WORDS, BANK_ROW_TILES * P], F32, tag="bank")
                for u in range(WORDS):
                    for rr in range(BANK_ROW_TILES):
                        first = (K_PASS // PAIR) * g + P * u
                        nc.tensor.transpose(
                            w_t[:, u, rr * P : (rr + 1) * P],
                            w_sb[n][:, BANK_ROW_TILES * rp + rr, :].bitcast(F32)[:, first : first + P],
                            ident_f[:],
                        )
                w_banks[(n, g, rp)] = w_t
            if g == PASSES - 1 and n + WEIGHT_BUFS < GROUPS:
                load_weights(n + WEIGHT_BUFS)

        def copy_out_weights(n, g, copies):
            grouped = gpool.tile([P, GROUP * PACK], BF16, align_bytes=64, tag="grouped")
            grouped_words = grouped[:].bitcast(F32).rearrange("p (f u) -> p f u", u=WORDS)
            bank_features = BANK_ROW_TILES * P
            for rp, copy in enumerate(copies):
                copy(
                    out=grouped_words[:, rp * bank_features : (rp + 1) * bank_features, :],
                    in_=w_banks[(n, g, rp)][:].rearrange("p u f -> p f u"),
                )
            grouped_w[(n, g)] = grouped

        def quantise_weights(n, g):
            if g == 0:
                codes = cpool.tile([P, PASSES, GROUP], U32, align_bytes=64)
                scales = cpool.tile([P, PASSES, GROUP], U8, align_bytes=64)
                w_codes[n] = codes
                w_scales[n] = scales
            nc.vector.quantize_mx(
                out=w_codes[n][:, g, :].bitcast(FP8X4), scales=w_scales[n][:, g, :],
                in_=grouped_w[(n, g)][:],
            )

        def project(n):
            for i in range(TOKEN_TILES):
                bank = ring.tile([P, GROUP], F32, tag="bank")
                for g in range(PASSES):
                    nc.tensor.matmul_mx(
                        out=bank[:],
                        lhsT=h_codes[:, i, g, :].bitcast(FP8X4),
                        lhsT_scale=h_scales[:, i, g, :],
                        rhs=w_codes[n][:, g, :].bitcast(FP8X4),
                        rhs_scale=w_scales[n][:, g, :],
                        start=(g == 0),
                        stop=(g == PASSES - 1),
                    )
                sums[(n, i)] = bank

        def add_bias(n, i):
            if i == 0:
                u = epool.tile([P, TOKEN_TILES, GROUP_HEADS, HEAD], F32)
                u_sb[n] = u
            nc.vector.tensor_tensor(
                out=u_sb[n][:, i, :, :].rearrange("p a d -> p (a d)"), in0=sums[(n, i)][:],
                in1=bias[:, n * GROUP : (n + 1) * GROUP], op=ALU.add,
            )

        def head_rms(n):
            ss = stats.tile([P, TOKEN_TILES * GROUP_HEADS], F32)
            for i in range(TOKEN_TILES):
                for head in range(GROUP_HEADS):
                    col = i * GROUP_HEADS + head
                    nc.scalar.activation(
                        out=squares[:, col * HEAD : (col + 1) * HEAD], in_=u_sb[n][:, i, head, :],
                        func=ACT.Square, accum_out=ss[:, col : col + 1],
                    )
            rms = stats.tile([P, TOKEN_TILES * GROUP_HEADS], F32)
            nc.scalar.activation(out=rms[:], in_=ss[:], func=ACT.Sqrt, scale=1.0 / HEAD, bias=eps[:, 0:1])
            rms_sb[n] = rms

        def invert_rms(n):
            inv = stats.tile([P, TOKEN_TILES * GROUP_HEADS], F32)
            nc.vector.reciprocal(out=inv[:], in_=rms_sb[n][:])
            rstd[n] = inv

        def rotate(n, rope):
            cos_gain, sin_gain = rope
            u = u_sb[n]
            shape = [P, TOKEN_TILES, GROUP_HEADS, HEAD]
            half_shape = [P, TOKEN_TILES, GROUP_HEADS, HALF]
            straight = epool.tile(shape, F32, bufs=3)
            nc.vector.tensor_tensor(
                out=straight[:], in0=u[:], in1=cos_gain[:].unsqueeze(2).to_broadcast(shape), op=ALU.mult
            )
            crossed = epool.tile(shape, F32)
            nc.vector.tensor_tensor(
                out=crossed[:, :, :, 0:HALF], in0=u[:, :, :, HALF:HEAD],
                in1=sin_gain[:, :, 0:HALF].unsqueeze(2).to_broadcast(half_shape), op=ALU.mult,
            )
            nc.vector.tensor_tensor(
                out=crossed[:, :, :, HALF:HEAD], in0=u[:, :, :, 0:HALF],
                in1=sin_gain[:, :, HALF:HEAD].unsqueeze(2).to_broadcast(half_shape), op=ALU.mult,
            )
            for i in range(TOKEN_TILES):
                nc.gpsimd.tensor_tensor(
                    out=straight[:, i, :, :], in0=straight[:, i, :, :], in1=crossed[:, i, :, :], op=ALU.add
                )
            rotated[n] = straight

        def scale_and_store(n):
            for i in range(TOKEN_TILES):
                for head in range(GROUP_HEADS):
                    col = i * GROUP_HEADS + head
                    nc.scalar.activation(
                        out=rotated[n][:, i, head, :], in_=rotated[n][:, i, head, :], func=ACT.Copy,
                        scale=rstd[n][:, col : col + 1],
                    )
                nc.sync.dma_start(
                    out=out_cols[n][i * P : (i + 1) * P, :],
                    in_=rotated[n][:, i, :, :].rearrange("p a d -> p (a d)"),
                )

        def store_plain(n):
            for i in range(TOKEN_TILES):
                nc.sync.dma_start(
                    out=out_cols[n][i * P : (i + 1) * P, :],
                    in_=u_sb[n][:, i, :, :].rearrange("p a d -> p (a d)"),
                )

        for i in range(TOKEN_TILES):
            x_stats(i)
        for i in range(TOKEN_TILES):
            if i >= RUN_AHEAD:
                x_copy_out(i - RUN_AHEAD)
            x_scale(i)
            x_transpose(i)
        for i in range(TOKEN_TILES - RUN_AHEAD, TOKEN_TILES):
            x_copy_out(i)

        assert TOKEN_TILES == PASSES
        for g in range(RUN_AHEAD):
            transpose_weights(0, g)
        for step in range(PASSES):
            copy_out_weights(0, step, (nc.scalar.copy, nc.vector.tensor_copy))
            if step + RUN_AHEAD < PASSES:
                transpose_weights(0, step + RUN_AHEAD)
            x_quantise(step)
        for g in range(PASSES):
            quantise_weights(0, g)

        rope = tables_to_psum(tables_q)
        for g in range(RUN_AHEAD):
            transpose_weights(1, g)
        for g in range(PASSES):
            copy_out_weights(1, g, (nc.scalar.copy, nc.scalar.copy))
            if g + RUN_AHEAD < PASSES:
                transpose_weights(1, g + RUN_AHEAD)
        project(0)

        for n in range(GROUPS):
            if n + 1 < GROUPS:
                for g in range(PASSES):
                    quantise_weights(n + 1, g)
            for i in range(TOKEN_TILES):
                add_bias(n, i)
            if n >= 1:
                invert_rms(n - 1)
            if n + 2 < GROUPS:
                for g in range(RUN_AHEAD):
                    transpose_weights(n + 2, g)
            if n == V_GROUP:
                store_plain(n)
            else:
                head_rms(n)
            if n + 2 < GROUPS:
                for g in range(PASSES):
                    first_copy = nc.vector.tensor_copy if g == 0 else nc.scalar.copy
                    copy_out_weights(n + 2, g, (first_copy, nc.scalar.copy))
                    if g + RUN_AHEAD < PASSES:
                        transpose_weights(n + 2, g + RUN_AHEAD)
            if n + 1 < GROUPS:
                project(n + 1)
            if n >= 1:
                scale_and_store(n - 1)
            if n != V_GROUP:
                rotate(n, rope)
            if n + 1 == K_GROUP:
                rope = tables_to_psum(tables_k)
